import numpy as np
import ml_dtypes


def mxq(x, axis, fmt="e4m3"):
    dtype, down = {"e4m3": (ml_dtypes.float8_e4m3fn, 7), "e5m2": (ml_dtypes.float8_e5m2, 14)}[fmt]
    v = np.moveaxis(np.asarray(x, np.float32).astype(ml_dtypes.bfloat16).astype(np.float64), axis, -1)
    blocks = v.reshape(v.shape[:-1] + (-1, 32))
    amax = np.abs(blocks).max(-1, keepdims=True)
    byte = np.maximum(np.where(amax > 0, np.frexp(amax)[1] - 1 + 127, 0) - down, 1)
    scale = np.exp2(byte - 127.0)
    codes = (blocks / scale).astype(np.float32).astype(dtype).astype(np.float64)
    return np.moveaxis((codes * scale).reshape(v.shape), -1, axis)


WIDE = False


def mx_kscale(k):
    if not WIDE:
        return np.ones(k)
    levels = np.array([20, -20, 10, -10, 0])
    if k % 512:
        return np.exp2(np.random.permutation(np.resize(levels, k // 32))).repeat(32)
    a = np.empty((k // 512, 16))
    for p in range(k // 512):
        a[p, :8] = np.random.permutation(np.resize(levels, 8))
        for g in range(8):
            far = levels[np.abs(levels - a[p, g]) >= 10]
            a[p, g + 8] = far[np.random.randint(len(far))]
    return np.exp2(a.ravel()).repeat(32)


BF16 = ml_dtypes.bfloat16


def bf(x):
    return np.asarray(x, np.float32).astype(BF16)


def f64(x):
    return np.asarray(x).astype(np.float64)


B, I, O, G = 512, 128, 1024, 3
K = I * G


def bspline_basis(d):
    inner = 1.0 - 6.0 * d * d + 6.0 * d * d * d
    outer = 2.0 * (1.0 - d) ** 3
    return np.where(d < 0.5, inner, np.where(d < 1.0, outer, np.zeros_like(d)))


def bspline_slope(d):
    inner = -12.0 * d + 18.0 * d * d
    outer = -6.0 * (1.0 - d) ** 2
    return np.where(d < 0.5, inner, np.where(d < 1.0, outer, np.zeros_like(d)))


def setup_inputs():
    g = np.linspace(-1.0, 1.0, G)
    s = mx_kscale(O)
    x_norm = np.tanh(np.random.standard_normal((B, I)))
    spline_weight = np.random.standard_normal((O, I, G)) / np.sqrt(I) / s[:, None, None]
    base_activation = np.random.standard_normal((O, I)) * 4.0 / np.sqrt(I) / s[:, None]
    grid_points = g + 0.1 * (g[1] - g[0]) * np.random.standard_normal(G)
    grad_out = np.random.standard_normal((B, O)) * np.exp2(np.random.randint(-12, 1, (B, 1))) * 4.0 * s
    return {"x_norm": bf(x_norm),
            "spline_weight": bf(spline_weight),
            "base_activation": bf(base_activation),
            "grid_points": bf(grid_points),
            "grad_out": bf(grad_out)}


def reference(x_norm, spline_weight, base_activation, grid_points, grad_out):
    t = f64(x_norm)
    diff = t[:, :, None] - f64(grid_points)
    slope = bspline_slope(np.abs(diff)) * np.sign(diff)
    gq = mxq(f64(grad_out), 1, "e5m2")
    h = gq @ mxq(f64(spline_weight).reshape(O, K), 0, "e4m3")
    base = gq @ mxq(f64(base_activation), 0, "e4m3")
    return (h.reshape(B, I, G) * slope).sum(axis=2) + 0.1 * base

@@ -1,0 +1,248 @@
+from contextlib import ExitStack
+
+import concourse.mybir as mybir
+from concourse.masks import make_identity
+
+F32 = mybir.dt.float32
+BF16 = mybir.dt.bfloat16
+U32 = mybir.dt.uint32
+U8 = mybir.dt.uint8
+E4M3_X4 = mybir.dt.float8_e4m3fn_x4
+E5M2_X4 = mybir.dt.float8_e5m2_x4
+ALU = mybir.AluOpType
+ACT = mybir.ActivationFunctionType
+
+P = 128
+B, I, O, G = 512, 128, 1024, 3
+PACK = 4
+K_PASS = P * PACK
+PASSES = O // K_PASS
+HALVES = 2
+ROW_TILES = B // P
+SPLINE_COLS = I * G
+W_COLS = SPLINE_COLS + I
+
+FLOPS = 2 * B * O * W_COLS
+
+
+def tile_advancedkanlayer_pa_s_kernel(
+    tc, x_norm, spline_weight, base_activation, grid_points, grad_out, out
+):
+    nc = tc.nc
+
+    spline_rows = spline_weight.rearrange("(c p j) i g -> p c (j i g)", c=PASSES, j=PACK)
+    base_rows = base_activation.rearrange("(c p j) i -> p c (j i)", c=PASSES, j=PACK)
+    x_rows = x_norm.rearrange("(p t) i -> p t i", t=ROW_TILES)
+    grad_rows = grad_out.rearrange("(p t) o -> p t o", t=ROW_TILES)
+    out_rows = out.rearrange("(p t) i -> p t i", t=ROW_TILES)
+
+    with tc.tile_pool(name="keep", bufs=1) as keep, tc.psum_pool(
+        name="flipped", bufs=ROW_TILES
+    ) as flipped, tc.psum_pool(name="sums", bufs=ROW_TILES) as sums, ExitStack() as written_order:
+        identity = keep.tile([P, P], F32)
+        make_identity(nc, identity[:])
+
+        written_order.enter_context(tc.manual_schedule())
+
+        x_bf = keep.tile([P, ROW_TILES, I], BF16)
+        nc.sync.dma_start(out=x_bf[:], in_=x_rows)
+        grid_bf = keep.tile([P, G], BF16)
+        nc.scalar.dma_start(out=grid_bf[:], in_=grid_points.partition_broadcast(P))
+
+        table_in = keep.tile([P, 1], F32)
+        table_out = keep.tile([P, 1], F32)
+        nc.gpsimd.memset(table_in[:], 0.0)
+        nc.scalar.activation(out=table_out[:], in_=table_in[:], func=ACT.Abs)
+
+        spline_raw = keep.tile([P, PASSES, PACK, SPLINE_COLS], BF16)
+        base_raw = keep.tile([P, PASSES, PACK, I], BF16)
+        for c in range(PASSES):
+            nc.sync.dma_start(
+                out=spline_raw[:, c].rearrange("p j w -> p (j w)"),
+                in_=spline_rows[:, c],
+            )
+            nc.sync.dma_start(
+                out=base_raw[:, c].rearrange("p j w -> p (j w)"),
+                in_=base_rows[:, c],
+            )
+        grad_raw = keep.tile([P, ROW_TILES, O], BF16)
+        for t in range(ROW_TILES):
+            nc.sync.dma_start(out=grad_raw[:, t, :], in_=grad_rows[:, t, :])
+
+        grid_minus_half = keep.tile([P, G], F32)
+        nc.vector.tensor_scalar(
+            out=grid_minus_half[:], in0=grid_bf[:], scalar1=-0.5, scalar2=None, op0=ALU.add
+        )
+
+        dist = keep.tile([P, ROW_TILES, G, I], F32)
+        minus_far = keep.tile([P, ROW_TILES, G, I], F32)
+        minus_near = keep.tile([P, ROW_TILES, G, I], F32)
+        six_q = keep.tile([P, ROW_TILES, G, I], F32)
+        fold_once = keep.tile([P, ROW_TILES, G, I], F32)
+        fold_twice = keep.tile([P, ROW_TILES, SPLINE_COLS], F32)
+        slope = keep.tile([P, ROW_TILES, G, I], F32)
+
+        w_grouped = keep.tile([P, PASSES, W_COLS, PACK], BF16, align_bytes=64)
+        w_codes = keep.tile([P, PASSES, W_COLS], U32, align_bytes=64)
+        w_scales = keep.tile([P, PASSES, W_COLS], U8, align_bytes=64)
+
+        def add_six_q_terms(g):
+            nc.vector.scalar_tensor_tensor(
+                out=six_q[:, :, g, :],
+                in0=minus_far[:, :, g, :],
+                scalar=12.0,
+                in1=minus_near[:, :, g, :],
+                op0=ALU.add,
+                op1=ALU.add,
+            )
+
+        def group_spline_rows(c):
+            nc.vector.tensor_copy(
+                out=w_grouped[:, c, 0:SPLINE_COLS, :].rearrange("p (w r) j -> p w j r", r=4),
+                in_=spline_raw[:, c].rearrange("p j (w r) -> p w j r", r=4),
+            )
+
+        def group_base_rows(c):
+            nc.scalar.copy(
+                out=w_grouped[:, c, SPLINE_COLS:W_COLS, :].rearrange("p (w r) j -> p w j r", r=4),
+                in_=base_raw[:, c].rearrange("p j (w r) -> p w j r", r=4),
+            )
+
+        for g in range(G):
+            nc.scalar.activation(
+                out=dist[:, :, g, :],
+                in_=x_bf[:],
+                func=ACT.Abs,
+                bias=grid_bf[:, g : g + 1],
+                scale=-1.0,
+            )
+            nc.vector.tensor_scalar(
+                out=minus_far[:, :, g, :],
+                in0=dist[:, :, g, :],
+                scalar1=-6.0,
+                scalar2=-6.0,
+                op0=ALU.mult,
+                op1=ALU.max,
+            )
+            nc.vector.tensor_scalar(
+                out=minus_near[:, :, g, :],
+                in0=dist[:, :, g, :],
+                scalar1=-12.0,
+                scalar2=-6.0,
+                op0=ALU.mult,
+                op1=ALU.max,
+            )
+            if g > 0:
+                add_six_q_terms(g - 1)
+        group_base_rows(0)
+        group_spline_rows(0)
+        add_six_q_terms(G - 1)
+        for g in range(G):
+            nc.scalar.activation(
+                out=fold_once[:, :, g, :],
+                in_=x_bf[:],
+                func=ACT.Abs,
+                bias=grid_minus_half[:, g : g + 1],
+                scale=-1.0,
+            )
+        group_base_rows(1)
+        group_spline_rows(1)
+        for c in range(PASSES):
+            nc.vector.quantize_mx(
+                out=w_codes[:, c, :].bitcast(E4M3_X4),
+                scales=w_scales[:, c, :],
+                in_=w_grouped[:, c].rearrange("p w j -> p (w j)"),
+            )
+
+        grad_grouped = keep.tile([P, ROW_TILES, PASSES * P * PACK], BF16, align_bytes=64)
+        grad_codes = keep.tile([P, ROW_TILES, PASSES * P], U32, align_bytes=64)
+        grad_scales = keep.tile([P, ROW_TILES, PASSES * P], U8, align_bytes=64)
+        for t in range(ROW_TILES):
+            grad_words = grad_raw[:, t, :].bitcast(F32)
+            words_t = flipped.tile([P, PASSES, HALVES, P], F32)
+            for c in range(PASSES):
+                for u in range(HALVES):
+                    first = c * HALVES * P + u
+                    nc.tensor.transpose(
+                        out=words_t[:, c, u, :],
+                        in_=grad_words[:, first : (c + 1) * HALVES * P : HALVES],
+                        identity=identity[:],
+                    )
+            nc.scalar.copy(
+                out=grad_grouped[:, t, :]
+                .bitcast(F32)
+                .rearrange("p (c b u) -> p c b u", c=PASSES, u=HALVES),
+                in_=words_t[:].rearrange("p c u b -> p c b u"),
+            )
+            nc.vector.quantize_mx(
+                out=grad_codes[:, t, :].bitcast(E5M2_X4),
+                scales=grad_scales[:, t, :],
+                in_=grad_grouped[:, t, :],
+            )
+            nc.scalar.activation(
+                out=fold_twice[:, t, :],
+                in_=fold_once[:, t].rearrange("p g i -> p (g i)"),
+                func=ACT.Abs,
+                bias=-1.0,
+                scale=1.0,
+            )
+            nc.vector.scalar_tensor_tensor(
+                out=slope[:, t].rearrange("p g i -> p (g i)"),
+                in0=fold_twice[:, t, :],
+                scalar=-0.5,
+                in1=six_q[:, t].rearrange("p g i -> p (g i)"),
+                op0=ALU.add,
+                op1=ALU.mult,
+            )
+
+        acc = []
+        for t in range(ROW_TILES):
+            acc.append(sums.tile([P, W_COLS], F32, name="acc"))
+            for c in range(PASSES):
+                rows = slice(c * P, (c + 1) * P)
+                nc.tensor.matmul_mx(
+                    out=acc[t][:],
+                    lhsT=grad_codes[:, t, rows].bitcast(E5M2_X4),
+                    lhsT_scale=grad_scales[:, t, rows],
+                    rhs=w_codes[:, c, :].bitcast(E4M3_X4),
+                    rhs_scale=w_scales[:, c, :],
+                    start=(c == 0),
+                    stop=(c == PASSES - 1),
+                )
+
+        weighted = keep.tile([P, ROW_TILES, G, I], F32)
+        first_two = keep.tile([P, ROW_TILES, I], F32)
+        third_and_base = keep.tile([P, ROW_TILES, I], F32)
+        out_sb = keep.tile([P, ROW_TILES, I], F32)
+        for pair in range(0, ROW_TILES, 2):
+            both = (pair, pair + 1)
+            for t in both:
+                nc.vector.tensor_tensor(
+                    out=weighted[:, t],
+                    in0=acc[t][:, 0:SPLINE_COLS].rearrange("p (i g) -> p g i", g=G),
+                    in1=slope[:, t],
+                    op=ALU.mult,
+                )
+            for t in both:
+                nc.vector.tensor_tensor(
+                    out=first_two[:, t, :],
+                    in0=weighted[:, t, 0, :],
+                    in1=weighted[:, t, 1, :],
+                    op=ALU.add,
+                )
+                nc.vector.scalar_tensor_tensor(
+                    out=third_and_base[:, t, :],
+                    in0=acc[t][:, SPLINE_COLS:W_COLS],
+                    scalar=0.1,
+                    in1=weighted[:, t, 2, :],
+                    op0=ALU.mult,
+                    op1=ALU.add,
+                )
+            for t in both:
+                nc.vector.tensor_tensor(
+                    out=out_sb[:, t, :],
+                    in0=first_two[:, t, :],
+                    in1=third_and_base[:, t, :],
+                    op=ALU.add,
+                )
+                nc.sync.dma_start(out=out_rows[:, t, :], in_=out_sb[:, t, :])

@@ -21,6 +21,7 @@ HALVES = 2
 ROW_TILES = B // P
 SPLINE_COLS = I * G
 W_COLS = SPLINE_COLS + I
+CUT = 256
 
 FLOPS = 2 * B * O * W_COLS
 
@@ -58,96 +59,97 @@ def tile_advancedkanlayer_pa_s_kernel(
         base_raw = keep.tile([P, PASSES, PACK, I], BF16)
         for c in range(PASSES):
             nc.sync.dma_start(
-                out=spline_raw[:, c].rearrange("p j w -> p (j w)"),
-                in_=spline_rows[:, c],
+                out=base_raw[:, c].rearrange("p j w -> p (j w)"), in_=base_rows[:, c]
             )
+        for c in range(PASSES):
             nc.sync.dma_start(
-                out=base_raw[:, c].rearrange("p j w -> p (j w)"),
-                in_=base_rows[:, c],
+                out=spline_raw[:, c].rearrange("p j w -> p (j w)"), in_=spline_rows[:, c]
             )
         grad_raw = keep.tile([P, ROW_TILES, O], BF16)
         for t in range(ROW_TILES):
             nc.sync.dma_start(out=grad_raw[:, t, :], in_=grad_rows[:, t, :])
 
-        grid_minus_half = keep.tile([P, G], F32)
+        grid_plus_half = keep.tile([P, G], F32)
         nc.vector.tensor_scalar(
-            out=grid_minus_half[:], in0=grid_bf[:], scalar1=-0.5, scalar2=None, op0=ALU.add
+            out=grid_plus_half[:], in0=grid_bf[:], scalar1=0.5, scalar2=None, op0=ALU.add
         )
 
-        dist = keep.tile([P, ROW_TILES, G, I], F32)
-        minus_far = keep.tile([P, ROW_TILES, G, I], F32)
-        minus_near = keep.tile([P, ROW_TILES, G, I], F32)
-        six_q = keep.tile([P, ROW_TILES, G, I], F32)
-        fold_once = keep.tile([P, ROW_TILES, G, I], F32)
-        fold_twice = keep.tile([P, ROW_TILES, SPLINE_COLS], F32)
-        slope = keep.tile([P, ROW_TILES, G, I], F32)
+        dist = keep.tile([P, G, ROW_TILES, I], F32)
+        near = keep.tile([P, G, ROW_TILES, I], F32)
+        kink = keep.tile([P, G, ROW_TILES, I], F32)
+        fold_once = keep.tile([P, G, ROW_TILES, I], F32)
+        fold_twice = keep.tile([P, ROW_TILES, G, I], F32)
 
         w_grouped = keep.tile([P, PASSES, W_COLS, PACK], BF16, align_bytes=64)
         w_codes = keep.tile([P, PASSES, W_COLS], U32, align_bytes=64)
         w_scales = keep.tile([P, PASSES, W_COLS], U8, align_bytes=64)
 
-        def add_six_q_terms(g):
-            nc.vector.scalar_tensor_tensor(
-                out=six_q[:, :, g, :],
-                in0=minus_far[:, :, g, :],
-                scalar=12.0,
-                in1=minus_near[:, :, g, :],
-                op0=ALU.add,
-                op1=ALU.add,
-            )
-
-        def group_spline_rows(c):
-            nc.vector.tensor_copy(
-                out=w_grouped[:, c, 0:SPLINE_COLS, :].rearrange("p (w r) j -> p w j r", r=4),
-                in_=spline_raw[:, c].rearrange("p j (w r) -> p w j r", r=4),
-            )
-
-        def group_base_rows(c):
-            nc.scalar.copy(
-                out=w_grouped[:, c, SPLINE_COLS:W_COLS, :].rearrange("p (w r) j -> p w j r", r=4),
-                in_=base_raw[:, c].rearrange("p j (w r) -> p w j r", r=4),
-            )
-
-        for g in range(G):
+        def distance(g):
             nc.scalar.activation(
-                out=dist[:, :, g, :],
+                out=dist[:, g],
                 in_=x_bf[:],
                 func=ACT.Abs,
                 bias=grid_bf[:, g : g + 1],
                 scale=-1.0,
             )
+
+        def clip_distance(g):
             nc.vector.tensor_scalar(
-                out=minus_far[:, :, g, :],
-                in0=dist[:, :, g, :],
-                scalar1=-6.0,
-                scalar2=-6.0,
-                op0=ALU.mult,
-                op1=ALU.max,
+                out=near[:, g],
+                in0=dist[:, g],
+                scalar1=1.0,
+                scalar2=0.5,
+                op0=ALU.min,
+                op1=ALU.subtract,
             )
-            nc.vector.tensor_scalar(
-                out=minus_near[:, :, g, :],
-                in0=dist[:, :, g, :],
-                scalar1=-12.0,
-                scalar2=-6.0,
+
+        def bend(g):
+            nc.vector.scalar_tensor_tensor(
+                out=kink[:, g],
+                in0=near[:, g],
+                scalar=3.0,
+                in1=near[:, g],
                 op0=ALU.mult,
-                op1=ALU.max,
+                op1=ALU.min,
             )
-            if g > 0:
-                add_six_q_terms(g - 1)
-        group_base_rows(0)
-        group_spline_rows(0)
-        add_six_q_terms(G - 1)
-        for g in range(G):
+
+        def fold_first(g):
             nc.scalar.activation(
-                out=fold_once[:, :, g, :],
+                out=fold_once[:, g],
                 in_=x_bf[:],
                 func=ACT.Abs,
-                bias=grid_minus_half[:, g : g + 1],
+                bias=grid_plus_half[:, g : g + 1],
                 scale=-1.0,
             )
-        group_base_rows(1)
-        group_spline_rows(1)
-        for c in range(PASSES):
+
+        def fold_second(t):
+            nc.scalar.activation(
+                out=fold_twice[:, t],
+                in_=fold_once[:, :, t, :],
+                func=ACT.Abs,
+                bias=-6.0,
+                scale=6.0,
+            )
+
+        def group_base_rows(c):
+            nc.vector.tensor_copy(
+                out=w_grouped[:, c, SPLINE_COLS:W_COLS, :].rearrange("p (w r) j -> p w j r", r=4),
+                in_=base_raw[:, c].rearrange("p j (w r) -> p w j r", r=4),
+            )
+
+        def group_spline_rows(c):
+            nc.vector.tensor_copy(
+                out=w_grouped[:, c, 0:CUT, :].rearrange("p (w r) j -> p w j r", r=4),
+                in_=spline_raw[:, c, :, 0:CUT].rearrange("p j (w r) -> p w j r", r=4),
+            )
+
+        def group_spline_rest(c):
+            nc.scalar.copy(
+                out=w_grouped[:, c, CUT:SPLINE_COLS, :].rearrange("p (w r) j -> p w j r", r=4),
+                in_=spline_raw[:, c, :, CUT:SPLINE_COLS].rearrange("p j (w r) -> p w j r", r=4),
+            )
+
+        def quantise_weights(c):
             nc.vector.quantize_mx(
                 out=w_codes[:, c, :].bitcast(E4M3_X4),
                 scales=w_scales[:, c, :],
@@ -157,9 +159,10 @@ def tile_advancedkanlayer_pa_s_kernel(
         grad_grouped = keep.tile([P, ROW_TILES, PASSES * P * PACK], BF16, align_bytes=64)
         grad_codes = keep.tile([P, ROW_TILES, PASSES * P], U32, align_bytes=64)
         grad_scales = keep.tile([P, ROW_TILES, PASSES * P], U8, align_bytes=64)
-        for t in range(ROW_TILES):
+
+        def transpose_grad(t):
             grad_words = grad_raw[:, t, :].bitcast(F32)
-            words_t = flipped.tile([P, PASSES, HALVES, P], F32)
+            words_t = flipped.tile([P, PASSES, HALVES, P], F32, name="words_t")
             for c in range(PASSES):
                 for u in range(HALVES):
                     first = c * HALVES * P + u
@@ -168,32 +171,49 @@ def tile_advancedkanlayer_pa_s_kernel(
                         in_=grad_words[:, first : (c + 1) * HALVES * P : HALVES],
                         identity=identity[:],
                     )
+            return words_t
+
+        def group_grad(t, words_t):
             nc.scalar.copy(
                 out=grad_grouped[:, t, :]
                 .bitcast(F32)
                 .rearrange("p (c b u) -> p c b u", c=PASSES, u=HALVES),
                 in_=words_t[:].rearrange("p c u b -> p c b u"),
             )
+
+        def quantise_grad(t):
             nc.vector.quantize_mx(
                 out=grad_codes[:, t, :].bitcast(E5M2_X4),
                 scales=grad_scales[:, t, :],
                 in_=grad_grouped[:, t, :],
             )
-            nc.scalar.activation(
-                out=fold_twice[:, t, :],
-                in_=fold_once[:, t].rearrange("p g i -> p (g i)"),
-                func=ACT.Abs,
-                bias=-1.0,
-                scale=1.0,
-            )
-            nc.vector.scalar_tensor_tensor(
-                out=slope[:, t].rearrange("p g i -> p (g i)"),
-                in0=fold_twice[:, t, :],
-                scalar=-0.5,
-                in1=six_q[:, t].rearrange("p g i -> p (g i)"),
-                op0=ALU.add,
-                op1=ALU.mult,
-            )
+
+        for g in range(G):
+            distance(g)
+        group_spline_rest(0)
+        group_spline_rest(1)
+        for g in range(G):
+            fold_first(g)
+        for t in range(ROW_TILES):
+            group_grad(t, transpose_grad(t))
+        for t in range(ROW_TILES):
+            fold_second(t)
+
+        group_base_rows(0)
+        group_base_rows(1)
+        clip_distance(0)
+        clip_distance(1)
+        bend(0)
+        clip_distance(2)
+        bend(1)
+        group_spline_rows(0)
+        bend(2)
+        group_spline_rows(1)
+        quantise_weights(0)
+        quantise_grad(0)
+        quantise_weights(1)
+        for t in range(1, ROW_TILES):
+            quantise_grad(t)
 
         acc = []
         for t in range(ROW_TILES):
@@ -210,39 +230,70 @@ def tile_advancedkanlayer_pa_s_kernel(
                     stop=(c == PASSES - 1),
                 )
 
+        times_zig = keep.tile([P, ROW_TILES, G, I], F32)
         weighted = keep.tile([P, ROW_TILES, G, I], F32)
         first_two = keep.tile([P, ROW_TILES, I], F32)
         third_and_base = keep.tile([P, ROW_TILES, I], F32)
         out_sb = keep.tile([P, ROW_TILES, I], F32)
-        for pair in range(0, ROW_TILES, 2):
-            both = (pair, pair + 1)
-            for t in both:
-                nc.vector.tensor_tensor(
-                    out=weighted[:, t],
-                    in0=acc[t][:, 0:SPLINE_COLS].rearrange("p (i g) -> p g i", g=G),
-                    in1=slope[:, t],
-                    op=ALU.mult,
-                )
-            for t in both:
-                nc.vector.tensor_tensor(
-                    out=first_two[:, t, :],
-                    in0=weighted[:, t, 0, :],
-                    in1=weighted[:, t, 1, :],
-                    op=ALU.add,
-                )
-                nc.vector.scalar_tensor_tensor(
-                    out=third_and_base[:, t, :],
-                    in0=acc[t][:, SPLINE_COLS:W_COLS],
-                    scalar=0.1,
-                    in1=weighted[:, t, 2, :],
-                    op0=ALU.mult,
-                    op1=ALU.add,
-                )
-            for t in both:
-                nc.vector.tensor_tensor(
-                    out=out_sb[:, t, :],
-                    in0=first_two[:, t, :],
-                    in1=third_and_base[:, t, :],
-                    op=ALU.add,
-                )
-                nc.sync.dma_start(out=out_rows[:, t, :], in_=out_sb[:, t, :])
+
+        def times_first_factor(t):
+            nc.vector.scalar_tensor_tensor(
+                out=times_zig[:, t],
+                in0=fold_twice[:, t],
+                scalar=-3.0,
+                in1=acc[t][:, 0:SPLINE_COLS].rearrange("p (i g) -> p g i", g=G),
+                op0=ALU.add,
+                op1=ALU.mult,
+            )
+
+        def times_second_factor(t):
+            nc.vector.scalar_tensor_tensor(
+                out=weighted[:, t],
+                in0=kink[:, :, t, :],
+                scalar=-0.5,
+                in1=times_zig[:, t],
+                op0=ALU.add,
+                op1=ALU.mult,
+            )
+
+        def add_pieces(t):
+            nc.vector.tensor_tensor(
+                out=first_two[:, t, :],
+                in0=weighted[:, t, 0, :],
+                in1=weighted[:, t, 1, :],
+                op=ALU.add,
+            )
+            nc.vector.scalar_tensor_tensor(
+                out=third_and_base[:, t, :],
+                in0=acc[t][:, SPLINE_COLS:W_COLS],
+                scalar=0.1,
+                in1=weighted[:, t, 2, :],
+                op0=ALU.mult,
+                op1=ALU.add,
+            )
+
+        def finish(t):
+            nc.vector.tensor_tensor(
+                out=out_sb[:, t, :],
+                in0=first_two[:, t, :],
+                in1=third_and_base[:, t, :],
+                op=ALU.add,
+            )
+            nc.sync.dma_start(out=out_rows[:, t, :], in_=out_sb[:, t, :])
+
+        times_first_factor(0)
+        times_first_factor(1)
+        times_second_factor(0)
+        times_first_factor(2)
+        times_second_factor(1)
+        add_pieces(0)
+        times_first_factor(3)
+        finish(0)
+        times_second_factor(2)
+        add_pieces(1)
+        times_second_factor(3)
+        finish(1)
+        add_pieces(2)
+        add_pieces(3)
+        finish(2)
+        finish(3)

@@ -21,7 +21,7 @@ HALVES = 2
 ROW_TILES = B // P
 SPLINE_COLS = I * G
 W_COLS = SPLINE_COLS + I
-CUT = 256
+CUT = 128
 
 FLOPS = 2 * B * O * W_COLS
 
@@ -57,17 +57,15 @@ def tile_advancedkanlayer_pa_s_kernel(
 
         spline_raw = keep.tile([P, PASSES, PACK, SPLINE_COLS], BF16)
         base_raw = keep.tile([P, PASSES, PACK, I], BF16)
-        for c in range(PASSES):
-            nc.sync.dma_start(
-                out=base_raw[:, c].rearrange("p j w -> p (j w)"), in_=base_rows[:, c]
-            )
+        nc.sync.dma_start(out=base_raw[:].rearrange("p c j w -> p c (j w)"), in_=base_rows)
         for c in range(PASSES):
             nc.sync.dma_start(
                 out=spline_raw[:, c].rearrange("p j w -> p (j w)"), in_=spline_rows[:, c]
             )
         grad_raw = keep.tile([P, ROW_TILES, O], BF16)
-        for t in range(ROW_TILES):
-            nc.sync.dma_start(out=grad_raw[:, t, :], in_=grad_rows[:, t, :])
+        for first in range(0, ROW_TILES, 2):
+            pair = slice(first, first + 2)
+            nc.sync.dma_start(out=grad_raw[:, pair, :], in_=grad_rows[:, pair, :])
 
         grid_plus_half = keep.tile([P, G], F32)
         nc.vector.tensor_scalar(
@@ -113,10 +111,10 @@ def tile_advancedkanlayer_pa_s_kernel(
                 op1=ALU.min,
             )
 
-        def fold_first(g):
+        def fold_first(g, tiles):
             nc.scalar.activation(
-                out=fold_once[:, g],
-                in_=x_bf[:],
+                out=fold_once[:, g, tiles, :],
+                in_=x_bf[:, tiles, :],
                 func=ACT.Abs,
                 bias=grid_plus_half[:, g : g + 1],
                 scale=-1.0,
@@ -192,12 +190,13 @@ def tile_advancedkanlayer_pa_s_kernel(
             distance(g)
         group_spline_rest(0)
         group_spline_rest(1)
-        for g in range(G):
-            fold_first(g)
         for t in range(ROW_TILES):
             group_grad(t, transpose_grad(t))
-        for t in range(ROW_TILES):
-            fold_second(t)
+        for first in range(0, ROW_TILES, 2):
+            for g in range(G):
+                fold_first(g, slice(first, first + 2))
+            for t in (first, first + 1):
+                fold_second(t)
 
         group_base_rows(0)
         group_base_rows(1)
@@ -230,7 +229,7 @@ def tile_advancedkanlayer_pa_s_kernel(
                     stop=(c == PASSES - 1),
                 )
 
-        times_zig = keep.tile([P, ROW_TILES, G, I], F32)
+        times_q = keep.tile([P, ROW_TILES, G, I], F32)
         weighted = keep.tile([P, ROW_TILES, G, I], F32)
         first_two = keep.tile([P, ROW_TILES, I], F32)
         third_and_base = keep.tile([P, ROW_TILES, I], F32)
@@ -238,9 +237,9 @@ def tile_advancedkanlayer_pa_s_kernel(
 
         def times_first_factor(t):
             nc.vector.scalar_tensor_tensor(
-                out=times_zig[:, t],
-                in0=fold_twice[:, t],
-                scalar=-3.0,
+                out=times_q[:, t],
+                in0=kink[:, :, t, :],
+                scalar=-0.5,
                 in1=acc[t][:, 0:SPLINE_COLS].rearrange("p (i g) -> p g i", g=G),
                 op0=ALU.add,
                 op1=ALU.mult,
@@ -249,9 +248,9 @@ def tile_advancedkanlayer_pa_s_kernel(
         def times_second_factor(t):
             nc.vector.scalar_tensor_tensor(
                 out=weighted[:, t],
-                in0=kink[:, :, t, :],
-                scalar=-0.5,
-                in1=times_zig[:, t],
+                in0=fold_twice[:, t],
+                scalar=-3.0,
+                in1=times_q[:, t],
                 op0=ALU.add,
                 op1=ALU.mult,
             )

@@ -21,7 +21,7 @@ HALVES = 2
 ROW_TILES = B // P
 SPLINE_COLS = I * G
 W_COLS = SPLINE_COLS + I
-CUT = 128
+CUT = 192
 
 FLOPS = 2 * B * O * W_COLS
 
@@ -57,15 +57,17 @@ def tile_advancedkanlayer_pa_s_kernel(
 
         spline_raw = keep.tile([P, PASSES, PACK, SPLINE_COLS], BF16)
         base_raw = keep.tile([P, PASSES, PACK, I], BF16)
-        nc.sync.dma_start(out=base_raw[:].rearrange("p c j w -> p c (j w)"), in_=base_rows)
+        for c in range(PASSES):
+            nc.sync.dma_start(
+                out=base_raw[:, c].rearrange("p j w -> p (j w)"), in_=base_rows[:, c]
+            )
         for c in range(PASSES):
             nc.sync.dma_start(
                 out=spline_raw[:, c].rearrange("p j w -> p (j w)"), in_=spline_rows[:, c]
             )
         grad_raw = keep.tile([P, ROW_TILES, O], BF16)
-        for first in range(0, ROW_TILES, 2):
-            pair = slice(first, first + 2)
-            nc.sync.dma_start(out=grad_raw[:, pair, :], in_=grad_rows[:, pair, :])
+        for tiles in (slice(0, 2), slice(2, ROW_TILES)):
+            nc.sync.dma_start(out=grad_raw[:, tiles, :], in_=grad_rows[:, tiles, :])
 
         grid_plus_half = keep.tile([P, G], F32)
         nc.vector.tensor_scalar(
@@ -190,13 +192,12 @@ def tile_advancedkanlayer_pa_s_kernel(
             distance(g)
         group_spline_rest(0)
         group_spline_rest(1)
+        for g in range(G):
+            fold_first(g, slice(0, 2))
         for t in range(ROW_TILES):
             group_grad(t, transpose_grad(t))
-        for first in range(0, ROW_TILES, 2):
-            for g in range(G):
-                fold_first(g, slice(first, first + 2))
-            for t in (first, first + 1):
-                fold_second(t)
+        fold_second(0)
+        fold_second(1)
 
         group_base_rows(0)
         group_base_rows(1)
@@ -280,18 +281,43 @@ def tile_advancedkanlayer_pa_s_kernel(
             )
             nc.sync.dma_start(out=out_rows[:, t, :], in_=out_sb[:, t, :])
 
+        tenth = keep.tile([P, ROW_TILES, I], F32)
+
+        def tenth_of_base(t):
+            nc.scalar.activation(
+                out=tenth[:, t, :], in_=acc[t][:, SPLINE_COLS:W_COLS], func=ACT.Copy, scale=0.1
+            )
+
+        def sum_on_tensor(t):
+            total = flipped.tile([P, PASSES, HALVES, P], F32, name="words_t")
+            pieces = [weighted[:, t, g, :] for g in range(G)] + [tenth[:, t, :]]
+            for n, piece in enumerate(pieces):
+                nc.tensor.matmul(
+                    out=total[:, 0, 0, :],
+                    lhsT=identity[:],
+                    rhs=piece,
+                    start=(n == 0),
+                    stop=(n == len(pieces) - 1),
+                )
+            nc.scalar.copy(out=out_sb[:, t, :], in_=total[:, 0, 0, :])
+            nc.scalar.dma_start(out=out_rows[:, t, :], in_=out_sb[:, t, :])
+
+        for g in range(G):
+            fold_first(g, slice(2, ROW_TILES))
         times_first_factor(0)
+        tenth_of_base(0)
         times_first_factor(1)
+        tenth_of_base(1)
+        fold_second(2)
+        fold_second(3)
         times_second_factor(0)
-        times_first_factor(2)
         times_second_factor(1)
-        add_pieces(0)
+        sum_on_tensor(0)
+        sum_on_tensor(1)
+        times_first_factor(2)
         times_first_factor(3)
-        finish(0)
         times_second_factor(2)
-        add_pieces(1)
         times_second_factor(3)
-        finish(1)
         add_pieces(2)
         add_pieces(3)
         finish(2)

@@ -307,15 +307,15 @@ def tile_advancedkanlayer_pa_s_kernel(
         times_first_factor(0)
         tenth_of_base(0)
         times_first_factor(1)
-        tenth_of_base(1)
         fold_second(2)
         fold_second(3)
         times_second_factor(0)
         times_second_factor(1)
         sum_on_tensor(0)
-        sum_on_tensor(1)
         times_first_factor(2)
+        add_pieces(1)
         times_first_factor(3)
+        finish(1)
         times_second_factor(2)
         times_second_factor(3)
         add_pieces(2)

@@ -61,12 +61,12 @@ def tile_advancedkanlayer_pa_s_kernel(
             nc.sync.dma_start(
                 out=base_raw[:, c].rearrange("p j w -> p (j w)"), in_=base_rows[:, c]
             )
+        grad_raw = keep.tile([P, ROW_TILES, O], BF16)
         for c in range(PASSES):
             nc.sync.dma_start(
                 out=spline_raw[:, c].rearrange("p j w -> p (j w)"), in_=spline_rows[:, c]
             )
-        grad_raw = keep.tile([P, ROW_TILES, O], BF16)
-        for tiles in (slice(0, 2), slice(2, ROW_TILES)):
+            tiles = slice(2 * c, 2 * c + 2)
             nc.sync.dma_start(out=grad_raw[:, tiles, :], in_=grad_rows[:, tiles, :])
 
         grid_plus_half = keep.tile([P, G], F32)
@@ -191,11 +191,13 @@ def tile_advancedkanlayer_pa_s_kernel(
         for g in range(G):
             distance(g)
         group_spline_rest(0)
+        fold_first(0, slice(0, 2))
+        fold_first(1, slice(0, 2))
         group_spline_rest(1)
-        for g in range(G):
-            fold_first(g, slice(0, 2))
         for t in range(ROW_TILES):
             group_grad(t, transpose_grad(t))
+        fold_first(2, slice(0, 2))
+        fold_first(0, slice(2, ROW_TILES))
         fold_second(0)
         fold_second(1)
 
@@ -302,8 +304,8 @@ def tile_advancedkanlayer_pa_s_kernel(
             nc.scalar.copy(out=out_sb[:, t, :], in_=total[:, 0, 0, :])
             nc.scalar.dma_start(out=out_rows[:, t, :], in_=out_sb[:, t, :])
 
-        for g in range(G):
-            fold_first(g, slice(2, ROW_TILES))
+        fold_first(1, slice(2, ROW_TILES))
+        fold_first(2, slice(2, ROW_TILES))
         times_first_factor(0)
         tenth_of_base(0)
         times_first_factor(1)

@@ -98,15 +98,15 @@ def tile_advancedkanlayer_pa_s_kernel(
                 out=near[:, g],
                 in0=dist[:, g],
                 scalar1=1.0,
-                scalar2=0.5,
+                scalar2=1.0,
                 op0=ALU.min,
-                op1=ALU.subtract,
+                op1=ALU.add,
             )
 
         def bend(g):
             nc.vector.scalar_tensor_tensor(
                 out=kink[:, g],
-                in0=near[:, g],
+                in0=dist[:, g],
                 scalar=3.0,
                 in1=near[:, g],
                 op0=ALU.mult,
@@ -242,7 +242,7 @@ def tile_advancedkanlayer_pa_s_kernel(
             nc.vector.scalar_tensor_tensor(
                 out=times_q[:, t],
                 in0=kink[:, :, t, :],
-                scalar=-0.5,
+                scalar=-2.0,
                 in1=acc[t][:, 0:SPLINE_COLS].rearrange("p (i g) -> p g i", g=G),
                 op0=ALU.add,
                 op1=ALU.mult,

@@ -194,8 +194,22 @@ def tile_advancedkanlayer_pa_s_kernel(
         fold_first(0, slice(0, 2))
         fold_first(1, slice(0, 2))
         group_spline_rest(1)
+        waking = sums.tile([P, W_COLS], F32, name="acc")
+
+        def wake():
+            nc.tensor.matmul(
+                out=waking[:, 0 : 2 * I],
+                lhsT=identity[:],
+                rhs=dist[:, 0, 0:2, :].rearrange("p t i -> p (t i)"),
+                start=True,
+                stop=True,
+            )
+
+        wake()
         for t in range(ROW_TILES):
             group_grad(t, transpose_grad(t))
+            if t == 1:
+                wake()
         fold_first(2, slice(0, 2))
         fold_first(0, slice(2, ROW_TILES))
         fold_second(0)

from contextlib import ExitStack

import concourse.mybir as mybir
from concourse.masks import make_identity

F32 = mybir.dt.float32
BF16 = mybir.dt.bfloat16
U32 = mybir.dt.uint32
U8 = mybir.dt.uint8
E4M3_X4 = mybir.dt.float8_e4m3fn_x4
E5M2_X4 = mybir.dt.float8_e5m2_x4
ALU = mybir.AluOpType
ACT = mybir.ActivationFunctionType

P = 128
B, I, O, G = 512, 128, 1024, 3
PACK = 4
K_PASS = P * PACK
PASSES = O // K_PASS
HALVES = 2
ROW_TILES = B // P
SPLINE_COLS = I * G
W_COLS = SPLINE_COLS + I
CUT = 192

FLOPS = 2 * B * O * W_COLS


def tile_advancedkanlayer_pa_s_kernel(
    tc, x_norm, spline_weight, base_activation, grid_points, grad_out, out
):
    nc = tc.nc

    spline_rows = spline_weight.rearrange("(c p j) i g -> p c (j i g)", c=PASSES, j=PACK)
    base_rows = base_activation.rearrange("(c p j) i -> p c (j i)", c=PASSES, j=PACK)
    x_rows = x_norm.rearrange("(p t) i -> p t i", t=ROW_TILES)
    grad_rows = grad_out.rearrange("(p t) o -> p t o", t=ROW_TILES)
    out_rows = out.rearrange("(p t) i -> p t i", t=ROW_TILES)

    with tc.tile_pool(name="keep", bufs=1) as keep, tc.psum_pool(
        name="flipped", bufs=ROW_TILES
    ) as flipped, tc.psum_pool(name="sums", bufs=ROW_TILES) as sums, ExitStack() as written_order:
        identity = keep.tile([P, P], F32)
        make_identity(nc, identity[:])

        written_order.enter_context(tc.manual_schedule())

        x_bf = keep.tile([P, ROW_TILES, I], BF16)
        nc.sync.dma_start(out=x_bf[:], in_=x_rows)
        grid_bf = keep.tile([P, G], BF16)
        nc.scalar.dma_start(out=grid_bf[:], in_=grid_points.partition_broadcast(P))

        table_in = keep.tile([P, 1], F32)
        table_out = keep.tile([P, 1], F32)
        nc.gpsimd.memset(table_in[:], 0.0)
        nc.scalar.activation(out=table_out[:], in_=table_in[:], func=ACT.Abs)

        spline_raw = keep.tile([P, PASSES, PACK, SPLINE_COLS], BF16)
        base_raw = keep.tile([P, PASSES, PACK, I], BF16)
        for c in range(PASSES):
            nc.sync.dma_start(
                out=base_raw[:, c].rearrange("p j w -> p (j w)"), in_=base_rows[:, c]
            )
        grad_raw = keep.tile([P, ROW_TILES, O], BF16)
        for c in range(PASSES):
            nc.sync.dma_start(
                out=spline_raw[:, c].rearrange("p j w -> p (j w)"), in_=spline_rows[:, c]
            )
            tiles = slice(2 * c, 2 * c + 2)
            nc.sync.dma_start(out=grad_raw[:, tiles, :], in_=grad_rows[:, tiles, :])

        grid_plus_half = keep.tile([P, G], F32)
        nc.vector.tensor_scalar(
            out=grid_plus_half[:], in0=grid_bf[:], scalar1=0.5, scalar2=None, op0=ALU.add
        )

        dist = keep.tile([P, G, ROW_TILES, I], F32)
        near = keep.tile([P, G, ROW_TILES, I], F32)
        kink = keep.tile([P, G, ROW_TILES, I], F32)
        fold_once = keep.tile([P, G, ROW_TILES, I], F32)
        fold_twice = keep.tile([P, ROW_TILES, G, I], F32)

        w_grouped = keep.tile([P, PASSES, W_COLS, PACK], BF16, align_bytes=64)
        w_codes = keep.tile([P, PASSES, W_COLS], U32, align_bytes=64)
        w_scales = keep.tile([P, PASSES, W_COLS], U8, align_bytes=64)

        def distance(g):
            nc.scalar.activation(
                out=dist[:, g],
                in_=x_bf[:],
                func=ACT.Abs,
                bias=grid_bf[:, g : g + 1],
                scale=-1.0,
            )

        def clip_distance(g):
            nc.vector.tensor_scalar(
                out=near[:, g],
                in0=dist[:, g],
                scalar1=1.0,
                scalar2=1.0,
                op0=ALU.min,
                op1=ALU.add,
            )

        def bend(g):
            nc.vector.scalar_tensor_tensor(
                out=kink[:, g],
                in0=dist[:, g],
                scalar=3.0,
                in1=near[:, g],
                op0=ALU.mult,
                op1=ALU.min,
            )

        def fold_first(g, tiles):
            nc.scalar.activation(
                out=fold_once[:, g, tiles, :],
                in_=x_bf[:, tiles, :],
                func=ACT.Abs,
                bias=grid_plus_half[:, g : g + 1],
                scale=-1.0,
            )

        def fold_second(t):
            nc.scalar.activation(
                out=fold_twice[:, t],
                in_=fold_once[:, :, t, :],
                func=ACT.Abs,
                bias=-6.0,
                scale=6.0,
            )

        def group_base_rows(c):
            nc.vector.tensor_copy(
                out=w_grouped[:, c, SPLINE_COLS:W_COLS, :].rearrange("p (w r) j -> p w j r", r=4),
                in_=base_raw[:, c].rearrange("p j (w r) -> p w j r", r=4),
            )

        def group_spline_rows(c):
            nc.vector.tensor_copy(
                out=w_grouped[:, c, 0:CUT, :].rearrange("p (w r) j -> p w j r", r=4),
                in_=spline_raw[:, c, :, 0:CUT].rearrange("p j (w r) -> p w j r", r=4),
            )

        def group_spline_rest(c):
            nc.scalar.copy(
                out=w_grouped[:, c, CUT:SPLINE_COLS, :].rearrange("p (w r) j -> p w j r", r=4),
                in_=spline_raw[:, c, :, CUT:SPLINE_COLS].rearrange("p j (w r) -> p w j r", r=4),
            )

        def quantise_weights(c):
            nc.vector.quantize_mx(
                out=w_codes[:, c, :].bitcast(E4M3_X4),
                scales=w_scales[:, c, :],
                in_=w_grouped[:, c].rearrange("p w j -> p (w j)"),
            )

        grad_grouped = keep.tile([P, ROW_TILES, PASSES * P * PACK], BF16, align_bytes=64)
        grad_codes = keep.tile([P, ROW_TILES, PASSES * P], U32, align_bytes=64)
        grad_scales = keep.tile([P, ROW_TILES, PASSES * P], U8, align_bytes=64)

        def transpose_grad(t):
            grad_words = grad_raw[:, t, :].bitcast(F32)
            words_t = flipped.tile([P, PASSES, HALVES, P], F32, name="words_t")
            for c in range(PASSES):
                for u in range(HALVES):
                    first = c * HALVES * P + u
                    nc.tensor.transpose(
                        out=words_t[:, c, u, :],
                        in_=grad_words[:, first : (c + 1) * HALVES * P : HALVES],
                        identity=identity[:],
                    )
            return words_t

        def group_grad(t, words_t):
            nc.scalar.copy(
                out=grad_grouped[:, t, :]
                .bitcast(F32)
                .rearrange("p (c b u) -> p c b u", c=PASSES, u=HALVES),
                in_=words_t[:].rearrange("p c u b -> p c b u"),
            )

        def quantise_grad(t):
            nc.vector.quantize_mx(
                out=grad_codes[:, t, :].bitcast(E5M2_X4),
                scales=grad_scales[:, t, :],
                in_=grad_grouped[:, t, :],
            )

        for g in range(G):
            distance(g)
        group_spline_rest(0)
        fold_first(0, slice(0, 2))
        fold_first(1, slice(0, 2))
        group_spline_rest(1)
        waking = sums.tile([P, W_COLS], F32, name="acc")

        def wake():
            nc.tensor.matmul(
                out=waking[:, 0 : 2 * I],
                lhsT=identity[:],
                rhs=dist[:, 0, 0:2, :].rearrange("p t i -> p (t i)"),
                start=True,
                stop=True,
            )

        wake()
        for t in range(ROW_TILES):
            group_grad(t, transpose_grad(t))
            if t == 1:
                wake()
        fold_first(2, slice(0, 2))
        fold_first(0, slice(2, ROW_TILES))
        fold_second(0)
        fold_second(1)

        group_base_rows(0)
        group_base_rows(1)
        clip_distance(0)
        clip_distance(1)
        bend(0)
        clip_distance(2)
        bend(1)
        group_spline_rows(0)
        bend(2)
        group_spline_rows(1)
        quantise_weights(0)
        quantise_grad(0)
        quantise_weights(1)
        for t in range(1, ROW_TILES):
            quantise_grad(t)

        acc = []
        for t in range(ROW_TILES):
            acc.append(sums.tile([P, W_COLS], F32, name="acc"))
            for c in range(PASSES):
                rows = slice(c * P, (c + 1) * P)
                nc.tensor.matmul_mx(
                    out=acc[t][:],
                    lhsT=grad_codes[:, t, rows].bitcast(E5M2_X4),
                    lhsT_scale=grad_scales[:, t, rows],
                    rhs=w_codes[:, c, :].bitcast(E4M3_X4),
                    rhs_scale=w_scales[:, c, :],
                    start=(c == 0),
                    stop=(c == PASSES - 1),
                )

        times_q = keep.tile([P, ROW_TILES, G, I], F32)
        weighted = keep.tile([P, ROW_TILES, G, I], F32)
        first_two = keep.tile([P, ROW_TILES, I], F32)
        third_and_base = keep.tile([P, ROW_TILES, I], F32)
        out_sb = keep.tile([P, ROW_TILES, I], F32)

        def times_first_factor(t):
            nc.vector.scalar_tensor_tensor(
                out=times_q[:, t],
                in0=kink[:, :, t, :],
                scalar=-2.0,
                in1=acc[t][:, 0:SPLINE_COLS].rearrange("p (i g) -> p g i", g=G),
                op0=ALU.add,
                op1=ALU.mult,
            )

        def times_second_factor(t):
            nc.vector.scalar_tensor_tensor(
                out=weighted[:, t],
                in0=fold_twice[:, t],
                scalar=-3.0,
                in1=times_q[:, t],
                op0=ALU.add,
                op1=ALU.mult,
            )

        def add_pieces(t):
            nc.vector.tensor_tensor(
                out=first_two[:, t, :],
                in0=weighted[:, t, 0, :],
                in1=weighted[:, t, 1, :],
                op=ALU.add,
            )
            nc.vector.scalar_tensor_tensor(
                out=third_and_base[:, t, :],
                in0=acc[t][:, SPLINE_COLS:W_COLS],
                scalar=0.1,
                in1=weighted[:, t, 2, :],
                op0=ALU.mult,
                op1=ALU.add,
            )

        def finish(t):
            nc.vector.tensor_tensor(
                out=out_sb[:, t, :],
                in0=first_two[:, t, :],
                in1=third_and_base[:, t, :],
                op=ALU.add,
            )
            nc.sync.dma_start(out=out_rows[:, t, :], in_=out_sb[:, t, :])

        tenth = keep.tile([P, ROW_TILES, I], F32)

        def tenth_of_base(t):
            nc.scalar.activation(
                out=tenth[:, t, :], in_=acc[t][:, SPLINE_COLS:W_COLS], func=ACT.Copy, scale=0.1
            )

        def sum_on_tensor(t):
            total = flipped.tile([P, PASSES, HALVES, P], F32, name="words_t")
            pieces = [weighted[:, t, g, :] for g in range(G)] + [tenth[:, t, :]]
            for n, piece in enumerate(pieces):
                nc.tensor.matmul(
                    out=total[:, 0, 0, :],
                    lhsT=identity[:],
                    rhs=piece,
                    start=(n == 0),
                    stop=(n == len(pieces) - 1),
                )
            nc.scalar.copy(out=out_sb[:, t, :], in_=total[:, 0, 0, :])
            nc.scalar.dma_start(out=out_rows[:, t, :], in_=out_sb[:, t, :])

        fold_first(1, slice(2, ROW_TILES))
        fold_first(2, slice(2, ROW_TILES))
        times_first_factor(0)
        tenth_of_base(0)
        times_first_factor(1)
        fold_second(2)
        fold_second(3)
        times_second_factor(0)
        times_second_factor(1)
        sum_on_tensor(0)
        times_first_factor(2)
        add_pieces(1)
        times_first_factor(3)
        finish(1)
        times_second_factor(2)
        times_second_factor(3)
        add_pieces(2)
        add_pieces(3)
        finish(2)
        finish(3)
